import numpy as np
import ml_dtypes


def mxq(x, axis, fmt="e4m3"):
    dtype, down = {"e4m3": (ml_dtypes.float8_e4m3fn, 7), "e5m2": (ml_dtypes.float8_e5m2, 14)}[fmt]
    v = np.moveaxis(np.asarray(x, np.float32).astype(ml_dtypes.bfloat16).astype(np.float64), axis, -1)
    blocks = v.reshape(v.shape[:-1] + (-1, 32))
    amax = np.abs(blocks).max(-1, keepdims=True)
    byte = np.maximum(np.where(amax > 0, np.frexp(amax)[1] - 1 + 127, 0) - down, 1)
    scale = np.exp2(byte - 127.0)
    codes = (blocks / scale).astype(np.float32).astype(dtype).astype(np.float64)
    return np.moveaxis((codes * scale).reshape(v.shape), -1, axis)


WIDE = False


def mx_kscale(k):
    if not WIDE:
        return np.ones(k)
    levels = np.array([10, -10, 5, -5, 0])
    a = np.random.permutation(np.resize(levels, k // 512 * 4)).reshape(k // 512, 4)
    idx = np.arange(k)
    return np.exp2(a[idx // 512, idx % 128 // 32])


BF16 = ml_dtypes.bfloat16


def bf(x):
    return np.asarray(x, np.float32).astype(BF16)


def f64(x):
    return np.asarray(x).astype(np.float64)


B, T, D, H = 8, 1024, 512, 128
N = B * T
EMA0 = 1.0


def sigmoid(v):
    return 1.0 / (1.0 + np.exp(-v))


def surprise_gate(err):
    err_mag = np.sqrt(np.sum(err * err)) / N
    ema = 0.95 * EMA0 + 0.05 * err_mag
    return np.minimum(err_mag / np.maximum(ema, 1e-8), 3.0)


def setup_inputs():
    s, t = mx_kscale(D), mx_kscale(N)
    return {"err": bf(np.random.standard_normal((N, D)) * 2.3 * s[None, :] * t[:, None]),
            "W_down": bf(np.random.standard_normal((D, H)) / np.sqrt(D) / s[:, None]),
            "gate_pre": bf(np.random.standard_normal((N, H))),
            "up_pre": bf(np.random.standard_normal((N, H))),
            "x_pred": bf(np.random.standard_normal((N, D)) / t[:, None])}


def reference(err, W_down, gate_pre, up_pre, x_pred):
    err, gate_pre, up_pre = f64(err), f64(gate_pre), f64(up_pre)
    sg = surprise_gate(err)
    d_h = mxq(err, 1, "e4m3") @ mxq(f64(W_down), 0, "e4m3")
    sig = sigmoid(gate_pre)
    gate_act = gate_pre * sig
    d_gate_act = d_h * up_pre
    d_up_val = d_h * gate_act
    d_gate_pre = d_gate_act * sig * (1.0 + gate_pre * (1.0 - sig))
    xq = mxq(f64(x_pred), 0, "e4m3")
    grad_gate = (mxq(d_gate_pre, 0, "e4m3").T @ xq) / N
    grad_up = (mxq(d_up_val, 0, "e4m3").T @ xq) / N
    return grad_up * sg, grad_gate * sg

@@ -1,0 +1,253 @@
+from contextlib import ExitStack
+
+import concourse.mybir as mybir
+from concourse.masks import make_identity
+
+F32 = mybir.dt.float32
+BF16 = mybir.dt.bfloat16
+U32 = mybir.dt.uint32
+U8 = mybir.dt.uint8
+FP8X4 = mybir.dt.float8_e4m3fn_x4
+ACT = mybir.ActivationFunctionType
+ALU = mybir.AluOpType
+AX = mybir.AxisListType
+
+P = 128
+PACK = 4
+K_PASS = P * PACK
+
+N_TOKENS = 8192
+D = 512
+H = 128
+GROUPS = 2
+CHUNK = GROUPS * K_PASS
+N_CHUNKS = N_TOKENS // CHUNK
+
+FLOPS = 3 * 2 * N_TOKENS * D * H
+
+
+def tile_continuummemorysystem_pa_t_kernel(
+    tc, err, W_down, gate_pre, up_pre, x_pred, out_0, out_1
+):
+    nc = tc.nc
+    with ExitStack() as ctx:
+        const = ctx.enter_context(tc.tile_pool(name="const", bufs=1))
+        inputs = ctx.enter_context(tc.tile_pool(name="inputs", bufs=3))
+        work = ctx.enter_context(tc.tile_pool(name="work", bufs=2))
+        mx = ctx.enter_context(tc.tile_pool(name="mx", bufs=2))
+        psum_t = ctx.enter_context(tc.psum_pool(name="psum_t", bufs=4))
+        psum_dh = ctx.enter_context(tc.psum_pool(name="psum_dh", bufs=2))
+        psum_acc = ctx.enter_context(tc.psum_pool(name="psum_acc", bufs=1))
+
+        ident = const.tile([P, P], F32)
+        make_identity(nc, ident[:])
+        ones = const.tile([P, P], F32)
+        nc.vector.memset(ones[:], 1.0)
+        half = const.tile([P, 1], F32)
+        nc.vector.memset(half[:], 0.5)
+        warm = const.tile([P, 1], F32)
+        nc.scalar.activation(out=warm[:], in_=half[:], func=ACT.Silu)
+
+        w_raw = const.tile([P, PACK, H], BF16)
+        for u in range(2):
+            nc.sync.dma_start(
+                out=w_raw[:, 2 * u : 2 * u + 2, :],
+                in_=W_down[256 * u : 256 * (u + 1), :].rearrange("(q e) h -> q e h", e=2),
+            )
+        w_grouped = const.tile([P, H, PACK], BF16, align_bytes=64)
+        nc.vector.tensor_copy(out=w_grouped[:], in_=w_raw[:].rearrange("q t h -> q h t"))
+        w_codes = const.tile([P, H], U32, align_bytes=64)
+        w_scales = const.tile([P, H], U8, align_bytes=64)
+        nc.vector.quantize_mx(
+            out=w_codes[:].bitcast(FP8X4),
+            scales=w_scales[:],
+            in_=w_grouped[:].rearrange("q h t -> q (h t)"),
+        )
+
+        sq_sums = const.tile([P, N_CHUNKS], F32)
+        acc_up = psum_acc.tile([P, D], F32)
+        acc_gate = psum_acc.tile([P, D], F32)
+
+        def token_rows(dram, c):
+            return dram[c * CHUNK : (c + 1) * CHUNK, :].rearrange(
+                "(g p j) f -> p g j f", p=P, j=PACK
+            )
+
+        def front(c):
+            err_sb = inputs.tile([P, GROUPS, PACK, D], BF16)
+            nc.sync.dma_start(out=err_sb[:], in_=token_rows(err, c))
+            gate_sb = inputs.tile([P, GROUPS, PACK, H], BF16)
+            nc.sync.dma_start(out=gate_sb[:], in_=token_rows(gate_pre, c))
+            up_sb = inputs.tile([P, GROUPS, PACK, H], BF16)
+            nc.sync.dma_start(out=up_sb[:], in_=token_rows(up_pre, c))
+            x_sb = inputs.tile([P, GROUPS, PACK, D], BF16)
+            nc.sync.dma_start(out=x_sb[:], in_=token_rows(x_pred, c))
+
+            err_words = err_sb[:].bitcast(F32)
+            err_grouped = work.tile([P, GROUPS, K_PASS, PACK], BF16, align_bytes=64)
+            grouped_words = err_grouped[:].bitcast(F32)
+            for g in range(GROUPS):
+                for pair in range(PACK // 2):
+                    err_t = psum_t.tile([P, 2, 2, P], F32)
+                    for jj in range(2):
+                        for u in range(2):
+                            nc.tensor.transpose(
+                                err_t[:, jj, u, :],
+                                err_words[:, g, 2 * pair + jj, u * P : (u + 1) * P],
+                                ident[:],
+                            )
+                    nc.scalar.copy(
+                        out=grouped_words[:, g, 2 * pair * P : 2 * (pair + 1) * P, :].rearrange(
+                            "q (jj p) u -> q jj p u", jj=2
+                        ),
+                        in_=err_t[:].rearrange("q jj u p -> q jj p u"),
+                    )
+
+            squares = work.tile([P, GROUPS * PACK * D], BF16)
+            nc.scalar.activation(
+                out=squares[:],
+                in_=err_sb[:].rearrange("p g j f -> p (g j f)"),
+                func=ACT.Square,
+                accum_out=sq_sums[:, c : c + 1],
+            )
+
+            tanh_half = work.tile([P, GROUPS, PACK, H], F32)
+            nc.scalar.activation(out=tanh_half[:], in_=gate_sb[:], func=ACT.Tanh, scale=0.5)
+            silu_neg = work.tile([P, GROUPS, PACK, H], F32)
+            nc.scalar.activation(out=silu_neg[:], in_=gate_sb[:], func=ACT.Silu, scale=-1.0)
+            neg_slope = work.tile([P, GROUPS, PACK, H], F32)
+            nc.vector.scalar_tensor_tensor(
+                out=neg_slope[:].rearrange("p g j h -> p (g j h)"),
+                in0=silu_neg[:].rearrange("p g j h -> p (g j h)"),
+                scalar=1.0,
+                in1=up_sb[:].rearrange("p g j h -> p (g j h)"),
+                op0=ALU.subtract,
+                op1=ALU.mult,
+            )
+
+            x_grouped = work.tile([P, GROUPS, D, PACK], BF16, align_bytes=64)
+            for g in range(GROUPS):
+                nc.vector.tensor_copy(
+                    out=x_grouped[:, g].rearrange("p (c i) j -> p c j i", i=4),
+                    in_=x_sb[:, g].rearrange("p j (c i) -> p c j i", i=4),
+                )
+            return {
+                "err_grouped": err_grouped,
+                "gate_sb": gate_sb,
+                "tanh_half": tanh_half,
+                "neg_slope": neg_slope,
+                "x_grouped": x_grouped,
+            }
+
+        def back(c, t):
+            err_codes = mx.tile([P, GROUPS * K_PASS], U32, align_bytes=64)
+            err_scales = mx.tile([P, GROUPS * K_PASS], U8, align_bytes=64)
+            nc.vector.quantize_mx(
+                out=err_codes[:].bitcast(FP8X4),
+                scales=err_scales[:],
+                in_=t["err_grouped"][:].rearrange("q g n s -> q (g n s)"),
+            )
+            x_codes = mx.tile([P, GROUPS, D], U32, align_bytes=64)
+            x_scales = mx.tile([P, GROUPS, D], U8, align_bytes=64)
+            nc.vector.quantize_mx(
+                out=x_codes[:].rearrange("p g d -> p (g d)").bitcast(FP8X4),
+                scales=x_scales[:].rearrange("p g d -> p (g d)"),
+                in_=t["x_grouped"][:].rearrange("p g d j -> p (g d j)"),
+            )
+
+            dh_sig2 = work.tile([P, GROUPS, PACK, H], F32)
+            d_grouped = work.tile([P, GROUPS, 2, H, PACK], BF16, align_bytes=64)
+            for g in range(GROUPS):
+                dh = psum_dh.tile([P, PACK, H], F32, tag="dh")
+                for j in range(PACK):
+                    cols = slice(g * K_PASS + j * P, g * K_PASS + (j + 1) * P)
+                    nc.tensor.matmul_mx(
+                        out=dh[:, j, :],
+                        lhsT=err_codes[:, cols].bitcast(FP8X4),
+                        lhsT_scale=err_scales[:, cols],
+                        rhs=w_codes[:].bitcast(FP8X4),
+                        rhs_scale=w_scales[:],
+                        start=True,
+                        stop=True,
+                    )
+                nc.vector.scalar_tensor_tensor(
+                    out=dh_sig2[:, g].rearrange("p j h -> p (j h)"),
+                    in0=t["tanh_half"][:, g].rearrange("p j h -> p (j h)"),
+                    scalar=1.0,
+                    in1=dh[:].rearrange("p j h -> p (j h)"),
+                    op0=ALU.add,
+                    op1=ALU.mult,
+                )
+                nc.vector.scalar_tensor_tensor(
+                    out=d_grouped[:, g, 0],
+                    in0=dh_sig2[:, g].rearrange("p j h -> p h j"),
+                    scalar=0.5,
+                    in1=t["gate_sb"][:, g].rearrange("p j h -> p h j"),
+                    op0=ALU.mult,
+                    op1=ALU.mult,
+                )
+                nc.vector.scalar_tensor_tensor(
+                    out=d_grouped[:, g, 1],
+                    in0=dh_sig2[:, g].rearrange("p j h -> p h j"),
+                    scalar=-0.5,
+                    in1=t["neg_slope"][:, g].rearrange("p j h -> p h j"),
+                    op0=ALU.mult,
+                    op1=ALU.mult,
+                )
+            d_codes = mx.tile([P, GROUPS, 2, H], U32, align_bytes=64)
+            d_scales = mx.tile([P, GROUPS, 2, H], U8, align_bytes=64)
+            nc.vector.quantize_mx(
+                out=d_codes[:].rearrange("p g o h -> p (g o h)").bitcast(FP8X4),
+                scales=d_scales[:].rearrange("p g o h -> p (g o h)"),
+                in_=d_grouped[:].rearrange("p g o h j -> p (g o h j)"),
+            )
+            for g in range(GROUPS):
+                first = c == 0 and g == 0
+                last = c == N_CHUNKS - 1 and g == GROUPS - 1
+                for o, acc in enumerate((acc_up, acc_gate)):
+                    nc.tensor.matmul_mx(
+                        out=acc[:],
+                        lhsT=d_codes[:, g, o, :].bitcast(FP8X4),
+                        lhsT_scale=d_scales[:, g, o, :],
+                        rhs=x_codes[:, g, :].bitcast(FP8X4),
+                        rhs_scale=x_scales[:, g, :],
+                        start=first,
+                        stop=last,
+                    )
+
+        tiles = {}
+        for c in range(N_CHUNKS + 1):
+            if c < N_CHUNKS:
+                tiles[c] = front(c)
+            if c >= 1:
+                back(c - 1, tiles[c - 1])
+
+        total_ps = psum_dh.tile([P, N_CHUNKS], F32, tag="dh")
+        nc.tensor.matmul(out=total_ps[:], lhsT=ones[:], rhs=sq_sums[:], start=True, stop=True)
+        total = const.tile([P, 1], F32)
+        nc.vector.tensor_reduce(out=total[:], in_=total_ps[:], axis=AX.X, op=ALU.add)
+        mag_sq = const.tile([P, 1], F32)
+        nc.vector.tensor_scalar_mul(out=mag_sq[:], in0=total[:], scalar1=1.0 / (N_TOKENS * N_TOKENS))
+        mag = const.tile([P, 1], F32)
+        nc.gpsimd.tensor_tensor(out=mag[:], in0=mag_sq[:], in1=half[:], op=ALU.pow)
+        ema = const.tile([P, 1], F32)
+        nc.vector.tensor_scalar(
+            out=ema[:], in0=mag[:], scalar1=0.05, scalar2=0.95, op0=ALU.mult, op1=ALU.add
+        )
+        ema_floor = const.tile([P, 1], F32)
+        nc.vector.tensor_scalar_max(out=ema_floor[:], in0=ema[:], scalar1=1e-8)
+        ema_inv = const.tile([P, 1], F32)
+        nc.vector.reciprocal(out=ema_inv[:], in_=ema_floor[:])
+        ratio = const.tile([P, 1], F32)
+        nc.vector.tensor_mul(out=ratio[:], in0=mag[:], in1=ema_inv[:])
+        gain = const.tile([P, 1], F32)
+        nc.vector.tensor_scalar(
+            out=gain[:], in0=ratio[:], scalar1=3.0, scalar2=1.0 / N_TOKENS, op0=ALU.min, op1=ALU.mult
+        )
+
+        res_up = const.tile([P, D], F32)
+        nc.scalar.activation(out=res_up[:], in_=acc_up[:], func=ACT.Copy, scale=gain[:, 0:1])
+        nc.sync.dma_start(out=out_0, in_=res_up[:])
+        res_gate = const.tile([P, D], F32)
+        nc.vector.tensor_scalar_mul(out=res_gate[:], in0=acc_gate[:], scalar1=gain[:, 0:1])
+        nc.sync.dma_start(out=out_1, in_=res_gate[:])

@@ -10,7 +10,6 @@ U8 = mybir.dt.uint8
 FP8X4 = mybir.dt.float8_e4m3fn_x4
 ACT = mybir.ActivationFunctionType
 ALU = mybir.AluOpType
-AX = mybir.AxisListType
 
 P = 128
 PACK = 4
@@ -19,11 +18,13 @@ K_PASS = P * PACK
 N_TOKENS = 8192
 D = 512
 H = 128
-GROUPS = 2
-CHUNK = GROUPS * K_PASS
-N_CHUNKS = N_TOKENS // CHUNK
+N_CHUNKS = N_TOKENS // K_PASS
 
 FLOPS = 3 * 2 * N_TOKENS * D * H
+
+SCALAR_AHEAD = 2
+X_AHEAD = 2
+LOAD_AHEAD = 1
 
 
 def tile_continuummemorysystem_pa_t_kernel(
@@ -32,30 +33,270 @@ def tile_continuummemorysystem_pa_t_kernel(
     nc = tc.nc
     with ExitStack() as ctx:
         const = ctx.enter_context(tc.tile_pool(name="const", bufs=1))
-        inputs = ctx.enter_context(tc.tile_pool(name="inputs", bufs=3))
+        inputs = ctx.enter_context(
+            tc.tile_pool(name="inputs", bufs=LOAD_AHEAD + SCALAR_AHEAD + 2)
+        )
+        early = ctx.enter_context(tc.tile_pool(name="early", bufs=SCALAR_AHEAD + 1))
+        x_mx = ctx.enter_context(tc.tile_pool(name="x_mx", bufs=X_AHEAD + 2))
         work = ctx.enter_context(tc.tile_pool(name="work", bufs=2))
-        mx = ctx.enter_context(tc.tile_pool(name="mx", bufs=2))
         psum_t = ctx.enter_context(tc.psum_pool(name="psum_t", bufs=4))
         psum_dh = ctx.enter_context(tc.psum_pool(name="psum_dh", bufs=2))
         psum_acc = ctx.enter_context(tc.psum_pool(name="psum_acc", bufs=1))
+        ctx.enter_context(tc.manual_schedule())
 
-        ident = const.tile([P, P], F32)
-        make_identity(nc, ident[:])
-        ones = const.tile([P, P], F32)
-        nc.vector.memset(ones[:], 1.0)
-        half = const.tile([P, 1], F32)
-        nc.vector.memset(half[:], 0.5)
-        warm = const.tile([P, 1], F32)
-        nc.scalar.activation(out=warm[:], in_=half[:], func=ACT.Silu)
+        chunks = {}
 
+        def token_rows(dram, c):
+            return dram[c * K_PASS : (c + 1) * K_PASS, :].rearrange("(p j) f -> p j f", j=PACK)
+
+        def load(c):
+            x_sb = inputs.tile([P, PACK, D], BF16)
+            nc.sync.dma_start(out=x_sb[:], in_=token_rows(x_pred, c))
+            gate_sb = inputs.tile([P, PACK, H], BF16)
+            nc.sync.dma_start(out=gate_sb[:], in_=token_rows(gate_pre, c))
+            err_sb = inputs.tile([P, PACK, D], BF16)
+            nc.sync.dma_start(out=err_sb[:], in_=token_rows(err, c))
+            up_sb = inputs.tile([P, PACK, H], BF16)
+            nc.sync.dma_start(out=up_sb[:], in_=token_rows(up_pre, c))
+            chunks[c] = {"gate_sb": gate_sb, "err_sb": err_sb, "x_sb": x_sb, "up_sb": up_sb}
+
+        def transpose_err(c):
+            t = chunks[c]
+            err_words = t["err_sb"][:].bitcast(F32)
+            for pair in range(PACK // 2):
+                err_t = psum_t.tile([P, 2, 2, P], F32, tag="err_t")
+                for jj in range(2):
+                    for u in range(2):
+                        nc.tensor.transpose(
+                            err_t[:, jj, u, :],
+                            err_words[:, 2 * pair + jj, u * P : (u + 1) * P],
+                            ident[:],
+                        )
+                t["err_t", pair] = err_t
+
+        def scalar_work(c):
+            if c < N_CHUNKS:
+                t = chunks[c]
+                silu_neg = early.tile([P, PACK, H], F32)
+                nc.scalar.activation(
+                    out=silu_neg[:], in_=t["gate_sb"][:], func=ACT.Silu, scale=-1.0
+                )
+                tanh_half = early.tile([P, PACK, H], F32)
+                nc.scalar.activation(
+                    out=tanh_half[:], in_=t["gate_sb"][:], func=ACT.Tanh, scale=0.5
+                )
+                err_grouped = early.tile([P, K_PASS, PACK], BF16, align_bytes=64)
+                grouped_words = err_grouped[:].bitcast(F32)
+                for pair in range(PACK // 2):
+                    nc.scalar.copy(
+                        out=grouped_words[:, 2 * pair * P : 2 * (pair + 1) * P, :].rearrange(
+                            "q (jj p) u -> q jj p u", jj=2
+                        ),
+                        in_=t["err_t", pair][:].rearrange("q jj u p -> q jj p u"),
+                    )
+                t["silu_neg"] = silu_neg
+                t["err_grouped"] = err_grouped
+                t["tanh_half"] = tanh_half
+            if c >= 1:
+                squares = work.tile([P, PACK * D], BF16)
+                nc.scalar.activation(
+                    out=squares[:],
+                    in_=chunks[c - 1]["err_sb"][:].rearrange("p j f -> p (j f)"),
+                    func=ACT.Square,
+                    accum_out=sq_sums[:, c - 1 : c],
+                )
+
+        def quantise_err(c):
+            t = chunks[c]
+            err_codes = work.tile([P, K_PASS], U32, align_bytes=64)
+            err_scales = work.tile([P, K_PASS], U8, align_bytes=64)
+            nc.vector.quantize_mx(
+                out=err_codes[:].bitcast(FP8X4),
+                scales=err_scales[:],
+                in_=t["err_grouped"][:].rearrange("q n s -> q (n s)"),
+            )
+            t["err_codes"] = err_codes
+            t["err_scales"] = err_scales
+
+        def first_matmul(c):
+            t = chunks[c]
+            dh = psum_dh.tile([P, PACK, H], F32)
+            for j in range(PACK):
+                cols = slice(j * P, (j + 1) * P)
+                nc.tensor.matmul_mx(
+                    out=dh[:, j, :],
+                    lhsT=t["err_codes"][:, cols].bitcast(FP8X4),
+                    lhsT_scale=t["err_scales"][:, cols],
+                    rhs=w_codes[:].bitcast(FP8X4),
+                    rhs_scale=w_scales[:],
+                    start=True,
+                    stop=True,
+                )
+            t["dh"] = dh
+
+        def regroup_x(c):
+            t = chunks[c]
+            x_grouped = work.tile([P, D, PACK], BF16, align_bytes=64)
+            nc.vector.tensor_copy(
+                out=x_grouped[:].rearrange("p (c i) j -> p c j i", i=4),
+                in_=t["x_sb"][:].rearrange("p j (c i) -> p c j i", i=4),
+            )
+            t["x_grouped"] = x_grouped
+
+        def quantise_x(c):
+            t = chunks[c]
+            x_codes = x_mx.tile([P, D], U32, align_bytes=64)
+            x_scales = x_mx.tile([P, D], U8, align_bytes=64)
+            nc.vector.quantize_mx(
+                out=x_codes[:].bitcast(FP8X4),
+                scales=x_scales[:],
+                in_=t["x_grouped"][:].rearrange("p d j -> p (d j)"),
+            )
+            t["x_codes"] = x_codes
+            t["x_scales"] = x_scales
+
+        def gate_slope(c):
+            t = chunks[c]
+            neg_slope = work.tile([P, PACK, H], F32)
+            nc.vector.scalar_tensor_tensor(
+                out=neg_slope[:].rearrange("p j h -> p (j h)"),
+                in0=t["silu_neg"][:].rearrange("p j h -> p (j h)"),
+                scalar=1.0,
+                in1=t["up_sb"][:].rearrange("p j h -> p (j h)"),
+                op0=ALU.subtract,
+                op1=ALU.mult,
+            )
+            t["neg_slope"] = neg_slope
+
+        def times_sigmoid(c):
+            t = chunks[c]
+            dh_sig2 = work.tile([P, PACK, H], F32)
+            nc.vector.scalar_tensor_tensor(
+                out=dh_sig2[:].rearrange("p j h -> p (j h)"),
+                in0=t["tanh_half"][:].rearrange("p j h -> p (j h)"),
+                scalar=1.0,
+                in1=t["dh"][:].rearrange("p j h -> p (j h)"),
+                op0=ALU.add,
+                op1=ALU.mult,
+            )
+            t["dh_sig2"] = dh_sig2
+            d_grouped = work.tile([P, 2, H, PACK], BF16, align_bytes=64)
+            t["d_grouped"] = d_grouped
+
+        def d_up_val(c):
+            t = chunks[c]
+            nc.vector.scalar_tensor_tensor(
+                out=t["d_grouped"][:, 0],
+                in0=t["dh_sig2"][:].rearrange("p j h -> p h j"),
+                scalar=0.5,
+                in1=t["gate_sb"][:].rearrange("p j h -> p h j"),
+                op0=ALU.mult,
+                op1=ALU.mult,
+            )
+
+        def d_gate_pre(c):
+            t = chunks[c]
+            nc.vector.scalar_tensor_tensor(
+                out=t["d_grouped"][:, 1],
+                in0=t["dh_sig2"][:].rearrange("p j h -> p h j"),
+                scalar=-0.5,
+                in1=t["neg_slope"][:].rearrange("p j h -> p h j"),
+                op0=ALU.mult,
+                op1=ALU.mult,
+            )
+
+        def quantise_d(c):
+            t = chunks[c]
+            d_codes = work.tile([P, 2, H], U32, align_bytes=64)
+            d_scales = work.tile([P, 2, H], U8, align_bytes=64)
+            nc.vector.quantize_mx(
+                out=d_codes[:].rearrange("p o h -> p (o h)").bitcast(FP8X4),
+                scales=d_scales[:].rearrange("p o h -> p (o h)"),
+                in_=t["d_grouped"][:].rearrange("p o h j -> p (o h j)"),
+            )
+            t["d_codes"] = d_codes
+            t["d_scales"] = d_scales
+
+        def second_matmuls(c):
+            t = chunks[c]
+            for o, acc in enumerate((acc_up, acc_gate)):
+                nc.tensor.matmul_mx(
+                    out=acc[:],
+                    lhsT=t["d_codes"][:, o, :].bitcast(FP8X4),
+                    lhsT_scale=t["d_scales"][:, o, :],
+                    rhs=t["x_codes"][:].bitcast(FP8X4),
+                    rhs_scale=t["x_scales"][:],
+                    start=(c == 0),
+                    stop=(c == N_CHUNKS - 1),
+                )
+
+        def surprise_gate():
+            total_ps = psum_t.tile([P, N_CHUNKS], F32, tag="err_t")
+            nc.tensor.matmul(out=total_ps[:], lhsT=ones[:], rhs=sq_sums[:], start=True, stop=True)
+            total_parts = const.tile([P, N_CHUNKS], F32)
+            mag_sq = const.tile([P, 1], F32)
+            nc.scalar.activation(
+                out=total_parts[:],
+                in_=total_ps[:],
+                func=ACT.Copy,
+                scale=1.0 / (N_TOKENS * N_TOKENS),
+                accum_out=mag_sq[:],
+            )
+            mag = const.tile([P, 1], F32)
+            nc.gpsimd.tensor_tensor(out=mag[:], in0=mag_sq[:], in1=half[:], op=ALU.pow)
+            ema = const.tile([P, 1], F32)
+            nc.gpsimd.tensor_scalar(
+                out=ema[:], in0=mag[:], scalar1=0.05, scalar2=0.95, op0=ALU.mult, op1=ALU.add
+            )
+            ema_floor = const.tile([P, 1], F32)
+            nc.gpsimd.tensor_scalar_max(out=ema_floor[:], in0=ema[:], scalar1=1e-8)
+            ema_inv = const.tile([P, 1], F32)
+            nc.gpsimd.tensor_tensor(out=ema_inv[:], in0=ema_floor[:], in1=minus_one[:], op=ALU.pow)
+            ratio = const.tile([P, 1], F32)
+            nc.gpsimd.tensor_tensor(out=ratio[:], in0=mag[:], in1=ema_inv[:], op=ALU.mult)
+            nc.gpsimd.tensor_scalar(
+                out=gain[:],
+                in0=ratio[:],
+                scalar1=3.0,
+                scalar2=1.0 / N_TOKENS,
+                op0=ALU.min,
+                op1=ALU.mult,
+            )
+
+        load(0)
         w_raw = const.tile([P, PACK, H], BF16)
         for u in range(2):
             nc.sync.dma_start(
                 out=w_raw[:, 2 * u : 2 * u + 2, :],
                 in_=W_down[256 * u : 256 * (u + 1), :].rearrange("(q e) h -> q e h", e=2),
             )
+        for c in range(1, SCALAR_AHEAD + LOAD_AHEAD):
+            load(c)
+
+        ident = const.tile([P, P], F32)
+        make_identity(nc, ident[:])
+        ones = const.tile([P, P], F32)
+        nc.gpsimd.memset(ones[:], 1.0)
+        half = const.tile([P, 1], F32)
+        nc.gpsimd.memset(half[:], 0.5)
+        minus_one = const.tile([P, 1], F32)
+        nc.gpsimd.memset(minus_one[:], -1.0)
+        warm = const.tile([P, 1], F32)
+        nc.scalar.activation(out=warm[:], in_=half[:], func=ACT.Silu)
+
+        sq_sums = const.tile([P, N_CHUNKS], F32)
+        gain = const.tile([P, 1], F32)
+        acc_up = psum_acc.tile([P, D], F32)
+        acc_gate = psum_acc.tile([P, D], F32)
+
+        for c in range(SCALAR_AHEAD):
+            transpose_err(c)
+            scalar_work(c)
+
+        regroup_x(0)
         w_grouped = const.tile([P, H, PACK], BF16, align_bytes=64)
         nc.vector.tensor_copy(out=w_grouped[:], in_=w_raw[:].rearrange("q t h -> q h t"))
+        quantise_x(0)
         w_codes = const.tile([P, H], U32, align_bytes=64)
         w_scales = const.tile([P, H], U8, align_bytes=64)
         nc.vector.quantize_mx(
@@ -63,187 +304,38 @@ def tile_continuummemorysystem_pa_t_kernel(
             scales=w_scales[:],
             in_=w_grouped[:].rearrange("q h t -> q (h t)"),
         )
+        for c in range(1, X_AHEAD):
+            regroup_x(c)
+            quantise_x(c)
+        quantise_err(0)
+        first_matmul(0)
 
-        sq_sums = const.tile([P, N_CHUNKS], F32)
-        acc_up = psum_acc.tile([P, D], F32)
-        acc_gate = psum_acc.tile([P, D], F32)
-
-        def token_rows(dram, c):
-            return dram[c * CHUNK : (c + 1) * CHUNK, :].rearrange(
-                "(g p j) f -> p g j f", p=P, j=PACK
-            )
-
-        def front(c):
-            err_sb = inputs.tile([P, GROUPS, PACK, D], BF16)
-            nc.sync.dma_start(out=err_sb[:], in_=token_rows(err, c))
-            gate_sb = inputs.tile([P, GROUPS, PACK, H], BF16)
-            nc.sync.dma_start(out=gate_sb[:], in_=token_rows(gate_pre, c))
-            up_sb = inputs.tile([P, GROUPS, PACK, H], BF16)
-            nc.sync.dma_start(out=up_sb[:], in_=token_rows(up_pre, c))
-            x_sb = inputs.tile([P, GROUPS, PACK, D], BF16)
-            nc.sync.dma_start(out=x_sb[:], in_=token_rows(x_pred, c))
-
-            err_words = err_sb[:].bitcast(F32)
-            err_grouped = work.tile([P, GROUPS, K_PASS, PACK], BF16, align_bytes=64)
-            grouped_words = err_grouped[:].bitcast(F32)
-            for g in range(GROUPS):
-                for pair in range(PACK // 2):
-                    err_t = psum_t.tile([P, 2, 2, P], F32)
-                    for jj in range(2):
-                        for u in range(2):
-                            nc.tensor.transpose(
-                                err_t[:, jj, u, :],
-                                err_words[:, g, 2 * pair + jj, u * P : (u + 1) * P],
-                                ident[:],
-                            )
-                    nc.scalar.copy(
-                        out=grouped_words[:, g, 2 * pair * P : 2 * (pair + 1) * P, :].rearrange(
-                            "q (jj p) u -> q jj p u", jj=2
-                        ),
-                        in_=err_t[:].rearrange("q jj u p -> q jj p u"),
-                    )
-
-            squares = work.tile([P, GROUPS * PACK * D], BF16)
-            nc.scalar.activation(
-                out=squares[:],
-                in_=err_sb[:].rearrange("p g j f -> p (g j f)"),
-                func=ACT.Square,
-                accum_out=sq_sums[:, c : c + 1],
-            )
-
-            tanh_half = work.tile([P, GROUPS, PACK, H], F32)
-            nc.scalar.activation(out=tanh_half[:], in_=gate_sb[:], func=ACT.Tanh, scale=0.5)
-            silu_neg = work.tile([P, GROUPS, PACK, H], F32)
-            nc.scalar.activation(out=silu_neg[:], in_=gate_sb[:], func=ACT.Silu, scale=-1.0)
-            neg_slope = work.tile([P, GROUPS, PACK, H], F32)
-            nc.vector.scalar_tensor_tensor(
-                out=neg_slope[:].rearrange("p g j h -> p (g j h)"),
-                in0=silu_neg[:].rearrange("p g j h -> p (g j h)"),
-                scalar=1.0,
-                in1=up_sb[:].rearrange("p g j h -> p (g j h)"),
-                op0=ALU.subtract,
-                op1=ALU.mult,
-            )
-
-            x_grouped = work.tile([P, GROUPS, D, PACK], BF16, align_bytes=64)
-            for g in range(GROUPS):
-                nc.vector.tensor_copy(
-                    out=x_grouped[:, g].rearrange("p (c i) j -> p c j i", i=4),
-                    in_=x_sb[:, g].rearrange("p j (c i) -> p c j i", i=4),
-                )
-            return {
-                "err_grouped": err_grouped,
-                "gate_sb": gate_sb,
-                "tanh_half": tanh_half,
-                "neg_slope": neg_slope,
-                "x_grouped": x_grouped,
-            }
-
-        def back(c, t):
-            err_codes = mx.tile([P, GROUPS * K_PASS], U32, align_bytes=64)
-            err_scales = mx.tile([P, GROUPS * K_PASS], U8, align_bytes=64)
-            nc.vector.quantize_mx(
-                out=err_codes[:].bitcast(FP8X4),
-                scales=err_scales[:],
-                in_=t["err_grouped"][:].rearrange("q g n s -> q (g n s)"),
-            )
-            x_codes = mx.tile([P, GROUPS, D], U32, align_bytes=64)
-            x_scales = mx.tile([P, GROUPS, D], U8, align_bytes=64)
-            nc.vector.quantize_mx(
-                out=x_codes[:].rearrange("p g d -> p (g d)").bitcast(FP8X4),
-                scales=x_scales[:].rearrange("p g d -> p (g d)"),
-                in_=t["x_grouped"][:].rearrange("p g d j -> p (g d j)"),
-            )
-
-            dh_sig2 = work.tile([P, GROUPS, PACK, H], F32)
-            d_grouped = work.tile([P, GROUPS, 2, H, PACK], BF16, align_bytes=64)
-            for g in range(GROUPS):
-                dh = psum_dh.tile([P, PACK, H], F32, tag="dh")
-                for j in range(PACK):
-                    cols = slice(g * K_PASS + j * P, g * K_PASS + (j + 1) * P)
-                    nc.tensor.matmul_mx(
-                        out=dh[:, j, :],
-                        lhsT=err_codes[:, cols].bitcast(FP8X4),
-                        lhsT_scale=err_scales[:, cols],
-                        rhs=w_codes[:].bitcast(FP8X4),
-                        rhs_scale=w_scales[:],
-                        start=True,
-                        stop=True,
-                    )
-                nc.vector.scalar_tensor_tensor(
-                    out=dh_sig2[:, g].rearrange("p j h -> p (j h)"),
-                    in0=t["tanh_half"][:, g].rearrange("p j h -> p (j h)"),
-                    scalar=1.0,
-                    in1=dh[:].rearrange("p j h -> p (j h)"),
-                    op0=ALU.add,
-                    op1=ALU.mult,
-                )
-                nc.vector.scalar_tensor_tensor(
-                    out=d_grouped[:, g, 0],
-                    in0=dh_sig2[:, g].rearrange("p j h -> p h j"),
-                    scalar=0.5,
-                    in1=t["gate_sb"][:, g].rearrange("p j h -> p h j"),
-                    op0=ALU.mult,
-                    op1=ALU.mult,
-                )
-                nc.vector.scalar_tensor_tensor(
-                    out=d_grouped[:, g, 1],
-                    in0=dh_sig2[:, g].rearrange("p j h -> p h j"),
-                    scalar=-0.5,
-                    in1=t["neg_slope"][:, g].rearrange("p j h -> p h j"),
-                    op0=ALU.mult,
-                    op1=ALU.mult,
-                )
-            d_codes = mx.tile([P, GROUPS, 2, H], U32, align_bytes=64)
-            d_scales = mx.tile([P, GROUPS, 2, H], U8, align_bytes=64)
-            nc.vector.quantize_mx(
-                out=d_codes[:].rearrange("p g o h -> p (g o h)").bitcast(FP8X4),
-                scales=d_scales[:].rearrange("p g o h -> p (g o h)"),
-                in_=d_grouped[:].rearrange("p g o h j -> p (g o h j)"),
-            )
-            for g in range(GROUPS):
-                first = c == 0 and g == 0
-                last = c == N_CHUNKS - 1 and g == GROUPS - 1
-                for o, acc in enumerate((acc_up, acc_gate)):
-                    nc.tensor.matmul_mx(
-                        out=acc[:],
-                        lhsT=d_codes[:, g, o, :].bitcast(FP8X4),
-                        lhsT_scale=d_scales[:, g, o, :],
-                        rhs=x_codes[:, g, :].bitcast(FP8X4),
-                        rhs_scale=x_scales[:, g, :],
-                        start=first,
-                        stop=last,
-                    )
-
-        tiles = {}
         for c in range(N_CHUNKS + 1):
-            if c < N_CHUNKS:
-                tiles[c] = front(c)
+            if c + SCALAR_AHEAD + LOAD_AHEAD < N_CHUNKS:
+                load(c + SCALAR_AHEAD + LOAD_AHEAD)
             if c >= 1:
-                back(c - 1, tiles[c - 1])
-
-        total_ps = psum_dh.tile([P, N_CHUNKS], F32, tag="dh")
-        nc.tensor.matmul(out=total_ps[:], lhsT=ones[:], rhs=sq_sums[:], start=True, stop=True)
-        total = const.tile([P, 1], F32)
-        nc.vector.tensor_reduce(out=total[:], in_=total_ps[:], axis=AX.X, op=ALU.add)
-        mag_sq = const.tile([P, 1], F32)
-        nc.vector.tensor_scalar_mul(out=mag_sq[:], in0=total[:], scalar1=1.0 / (N_TOKENS * N_TOKENS))
-        mag = const.tile([P, 1], F32)
-        nc.gpsimd.tensor_tensor(out=mag[:], in0=mag_sq[:], in1=half[:], op=ALU.pow)
-        ema = const.tile([P, 1], F32)
-        nc.vector.tensor_scalar(
-            out=ema[:], in0=mag[:], scalar1=0.05, scalar2=0.95, op0=ALU.mult, op1=ALU.add
-        )
-        ema_floor = const.tile([P, 1], F32)
-        nc.vector.tensor_scalar_max(out=ema_floor[:], in0=ema[:], scalar1=1e-8)
-        ema_inv = const.tile([P, 1], F32)
-        nc.vector.reciprocal(out=ema_inv[:], in_=ema_floor[:])
-        ratio = const.tile([P, 1], F32)
-        nc.vector.tensor_mul(out=ratio[:], in0=mag[:], in1=ema_inv[:])
-        gain = const.tile([P, 1], F32)
-        nc.vector.tensor_scalar(
-            out=gain[:], in0=ratio[:], scalar1=3.0, scalar2=1.0 / N_TOKENS, op0=ALU.min, op1=ALU.mult
-        )
+                quantise_d(c - 1)
+                second_matmuls(c - 1)
+            if c + SCALAR_AHEAD < N_CHUNKS:
+                transpose_err(c + SCALAR_AHEAD)
+            if c + SCALAR_AHEAD <= N_CHUNKS:
+                scalar_work(c + SCALAR_AHEAD)
+            if c + SCALAR_AHEAD == N_CHUNKS:
+                surprise_gate()
+            if c < N_CHUNKS:
+                times_sigmoid(c)
+                gate_slope(c)
+            if c + 1 < N_CHUNKS:
+                quantise_err(c + 1)
+                first_matmul(c + 1)
+            if c < N_CHUNKS:
+                d_up_val(c)
+            if c + X_AHEAD < N_CHUNKS:
+                regroup_x(c + X_AHEAD)
+            if c < N_CHUNKS:
+                d_gate_pre(c)
+            if c + X_AHEAD < N_CHUNKS:
+                quantise_x(c + X_AHEAD)
 
         res_up = const.tile([P, D], F32)
         nc.scalar.activation(out=res_up[:], in_=acc_up[:], func=ACT.Copy, scale=gain[:, 0:1])

@@ -22,9 +22,12 @@ N_CHUNKS = N_TOKENS // K_PASS
 
 FLOPS = 3 * 2 * N_TOKENS * D * H
 
-SCALAR_AHEAD = 2
+SCALAR_AHEAD = 3
 X_AHEAD = 2
-LOAD_AHEAD = 1
+LOAD_AHEAD = 2
+SQUARES_LATE = 3
+GRAM = P
+X_SHARE = 96
 
 
 def tile_continuummemorysystem_pa_t_kernel(
@@ -36,12 +39,14 @@ def tile_continuummemorysystem_pa_t_kernel(
         inputs = ctx.enter_context(
             tc.tile_pool(name="inputs", bufs=LOAD_AHEAD + SCALAR_AHEAD + 2)
         )
+        err_in = ctx.enter_context(
+            tc.tile_pool(name="err_in", bufs=LOAD_AHEAD + SQUARES_LATE + 2)
+        )
         early = ctx.enter_context(tc.tile_pool(name="early", bufs=SCALAR_AHEAD + 1))
         x_mx = ctx.enter_context(tc.tile_pool(name="x_mx", bufs=X_AHEAD + 2))
         work = ctx.enter_context(tc.tile_pool(name="work", bufs=2))
         psum_t = ctx.enter_context(tc.psum_pool(name="psum_t", bufs=4))
-        psum_dh = ctx.enter_context(tc.psum_pool(name="psum_dh", bufs=2))
-        psum_acc = ctx.enter_context(tc.psum_pool(name="psum_acc", bufs=1))
+        psum_one = ctx.enter_context(tc.psum_pool(name="psum_one", bufs=1))
         ctx.enter_context(tc.manual_schedule())
 
         chunks = {}
@@ -49,12 +54,18 @@ def tile_continuummemorysystem_pa_t_kernel(
         def token_rows(dram, c):
             return dram[c * K_PASS : (c + 1) * K_PASS, :].rearrange("(p j) f -> p j f", j=PACK)
 
+        def side_by_side(grouped, rows):
+            return (
+                grouped.rearrange("p (c i) j -> p c j i", i=4),
+                rows.rearrange("p j (c i) -> p c j i", i=4),
+            )
+
         def load(c):
             x_sb = inputs.tile([P, PACK, D], BF16)
             nc.sync.dma_start(out=x_sb[:], in_=token_rows(x_pred, c))
             gate_sb = inputs.tile([P, PACK, H], BF16)
             nc.sync.dma_start(out=gate_sb[:], in_=token_rows(gate_pre, c))
-            err_sb = inputs.tile([P, PACK, D], BF16)
+            err_sb = err_in.tile([P, PACK, D], BF16)
             nc.sync.dma_start(out=err_sb[:], in_=token_rows(err, c))
             up_sb = inputs.tile([P, PACK, H], BF16)
             nc.sync.dma_start(out=up_sb[:], in_=token_rows(up_pre, c))
@@ -73,18 +84,52 @@ def tile_continuummemorysystem_pa_t_kernel(
                             ident[:],
                         )
                 t["err_t", pair] = err_t
+            for j in range(PACK):
+                nc.tensor.matmul(
+                    out=gram[:],
+                    lhsT=t["err_sb"][:, j, 0:GRAM],
+                    rhs=t["err_sb"][:, j, 0:GRAM],
+                    start=(c == 0 and j == 0),
+                    stop=(c == N_CHUNKS - 1 and j == PACK - 1),
+                )
+
+        def scalar_regroup_x(c):
+            t = chunks[c]
+            x_grouped = early.tile([P, D, PACK], BF16, align_bytes=64)
+            to_view, from_view = side_by_side(
+                x_grouped[:, 0:X_SHARE, :], t["x_sb"][:, :, 0:X_SHARE]
+            )
+            nc.scalar.copy(out=to_view, in_=from_view)
+            t["x_grouped"] = x_grouped
+
+        def square_err(c):
+            squares = work.tile([P, PACK, D - GRAM], BF16)
+            nc.scalar.activation(
+                out=squares[:],
+                in_=chunks[c]["err_sb"][:, :, GRAM:D],
+                func=ACT.Square,
+                accum_out=sq_sums[:, c : c + 1],
+            )
 
         def scalar_work(c):
             if c < N_CHUNKS:
                 t = chunks[c]
-                silu_neg = early.tile([P, PACK, H], F32)
+                silu_neg = early.tile([P, H, PACK], F32)
                 nc.scalar.activation(
-                    out=silu_neg[:], in_=t["gate_sb"][:], func=ACT.Silu, scale=-1.0
+                    out=silu_neg[:],
+                    in_=t["gate_sb"][:].rearrange("p j h -> p h j"),
+                    func=ACT.Silu,
+                    scale=-1.0,
                 )
-                tanh_half = early.tile([P, PACK, H], F32)
+                tanh_half = early.tile([P, H, PACK], F32)
                 nc.scalar.activation(
-                    out=tanh_half[:], in_=t["gate_sb"][:], func=ACT.Tanh, scale=0.5
+                    out=tanh_half[:],
+                    in_=t["gate_sb"][:].rearrange("p j h -> p h j"),
+                    func=ACT.Tanh,
+                    scale=0.5,
                 )
+                if c + 1 < N_CHUNKS:
+                    scalar_regroup_x(c + 1)
                 err_grouped = early.tile([P, K_PASS, PACK], BF16, align_bytes=64)
                 grouped_words = err_grouped[:].bitcast(F32)
                 for pair in range(PACK // 2):
@@ -97,14 +142,8 @@ def tile_continuummemorysystem_pa_t_kernel(
                 t["silu_neg"] = silu_neg
                 t["err_grouped"] = err_grouped
                 t["tanh_half"] = tanh_half
-            if c >= 1:
-                squares = work.tile([P, PACK * D], BF16)
-                nc.scalar.activation(
-                    out=squares[:],
-                    in_=chunks[c - 1]["err_sb"][:].rearrange("p j f -> p (j f)"),
-                    func=ACT.Square,
-                    accum_out=sq_sums[:, c - 1 : c],
-                )
+            if c >= SQUARES_LATE:
+                square_err(c - SQUARES_LATE)
 
         def quantise_err(c):
             t = chunks[c]
@@ -120,7 +159,7 @@ def tile_continuummemorysystem_pa_t_kernel(
 
         def first_matmul(c):
             t = chunks[c]
-            dh = psum_dh.tile([P, PACK, H], F32)
+            dh = psum_one.tile([P, PACK, H], F32)
             for j in range(PACK):
                 cols = slice(j * P, (j + 1) * P)
                 nc.tensor.matmul_mx(
@@ -136,12 +175,10 @@ def tile_continuummemorysystem_pa_t_kernel(
 
         def regroup_x(c):
             t = chunks[c]
-            x_grouped = work.tile([P, D, PACK], BF16, align_bytes=64)
-            nc.vector.tensor_copy(
-                out=x_grouped[:].rearrange("p (c i) j -> p c j i", i=4),
-                in_=t["x_sb"][:].rearrange("p j (c i) -> p c j i", i=4),
+            to_view, from_view = side_by_side(
+                t["x_grouped"][:, X_SHARE:D, :], t["x_sb"][:, :, X_SHARE:D]
             )
-            t["x_grouped"] = x_grouped
+            nc.vector.tensor_copy(out=to_view, in_=from_view)
 
         def quantise_x(c):
             t = chunks[c]
@@ -157,12 +194,12 @@ def tile_continuummemorysystem_pa_t_kernel(
 
         def gate_slope(c):
             t = chunks[c]
-            neg_slope = work.tile([P, PACK, H], F32)
+            neg_slope = work.tile([P, H, PACK], F32)
             nc.vector.scalar_tensor_tensor(
-                out=neg_slope[:].rearrange("p j h -> p (j h)"),
-                in0=t["silu_neg"][:].rearrange("p j h -> p (j h)"),
+                out=neg_slope[:],
+                in0=t["silu_neg"][:],
                 scalar=1.0,
-                in1=t["up_sb"][:].rearrange("p j h -> p (j h)"),
+                in1=t["up_sb"][:].rearrange("p j h -> p h j"),
                 op0=ALU.subtract,
                 op1=ALU.mult,
             )
@@ -170,12 +207,12 @@ def tile_continuummemorysystem_pa_t_kernel(
 
         def times_sigmoid(c):
             t = chunks[c]
-            dh_sig2 = work.tile([P, PACK, H], F32)
+            dh_sig2 = work.tile([P, H, PACK], F32)
             nc.vector.scalar_tensor_tensor(
-                out=dh_sig2[:].rearrange("p j h -> p (j h)"),
-                in0=t["tanh_half"][:].rearrange("p j h -> p (j h)"),
+                out=dh_sig2[:],
+                in0=t["tanh_half"][:],
                 scalar=1.0,
-                in1=t["dh"][:].rearrange("p j h -> p (j h)"),
+                in1=t["dh"][:].rearrange("p j h -> p h j"),
                 op0=ALU.add,
                 op1=ALU.mult,
             )
@@ -187,7 +224,7 @@ def tile_continuummemorysystem_pa_t_kernel(
             t = chunks[c]
             nc.vector.scalar_tensor_tensor(
                 out=t["d_grouped"][:, 0],
-                in0=t["dh_sig2"][:].rearrange("p j h -> p h j"),
+                in0=t["dh_sig2"][:],
                 scalar=0.5,
                 in1=t["gate_sb"][:].rearrange("p j h -> p h j"),
                 op0=ALU.mult,
@@ -198,9 +235,9 @@ def tile_continuummemorysystem_pa_t_kernel(
             t = chunks[c]
             nc.vector.scalar_tensor_tensor(
                 out=t["d_grouped"][:, 1],
-                in0=t["dh_sig2"][:].rearrange("p j h -> p h j"),
+                in0=t["dh_sig2"][:],
                 scalar=-0.5,
-                in1=t["neg_slope"][:].rearrange("p j h -> p h j"),
+                in1=t["neg_slope"][:],
                 op0=ALU.mult,
                 op1=ALU.mult,
             )
@@ -230,10 +267,22 @@ def tile_continuummemorysystem_pa_t_kernel(
                     stop=(c == N_CHUNKS - 1),
                 )
 
+        def gram_diagonal():
+            diagonal = const.tile([P, GRAM], F32)
+            nc.vector.tensor_tensor(out=diagonal[:], in0=gram[:], in1=ident[:], op=ALU.mult)
+            nc.vector.tensor_reduce(
+                out=sq_sums[:, N_CHUNKS : N_CHUNKS + 1],
+                in_=diagonal[:],
+                axis=mybir.AxisListType.X,
+                op=ALU.add,
+            )
+
         def surprise_gate():
-            total_ps = psum_t.tile([P, N_CHUNKS], F32, tag="err_t")
-            nc.tensor.matmul(out=total_ps[:], lhsT=ones[:], rhs=sq_sums[:], start=True, stop=True)
-            total_parts = const.tile([P, N_CHUNKS], F32)
+            total_ps = psum_t.tile([P, N_CHUNKS + 1], F32, tag="err_t")
+            nc.tensor.matmul(
+                out=total_ps[:], lhsT=ones[:], rhs=sq_sums[:, 0 : N_CHUNKS + 1], start=True, stop=True
+            )
+            total_parts = const.tile([P, N_CHUNKS + 1], F32)
             mag_sq = const.tile([P, 1], F32)
             nc.scalar.activation(
                 out=total_parts[:],
@@ -284,14 +333,15 @@ def tile_continuummemorysystem_pa_t_kernel(
         warm = const.tile([P, 1], F32)
         nc.scalar.activation(out=warm[:], in_=half[:], func=ACT.Silu)
 
-        sq_sums = const.tile([P, N_CHUNKS], F32)
+        sq_sums = const.tile([P, N_CHUNKS + 8], F32)
         gain = const.tile([P, 1], F32)
-        acc_up = psum_acc.tile([P, D], F32)
-        acc_gate = psum_acc.tile([P, D], F32)
+        acc_up = psum_one.tile([P, D], F32)
+        acc_gate = psum_one.tile([P, D], F32)
+        gram = psum_one.tile([P, GRAM], F32)
 
-        for c in range(SCALAR_AHEAD):
-            transpose_err(c)
-            scalar_work(c)
+        scalar_regroup_x(0)
+        transpose_err(0)
+        scalar_work(0)
 
         regroup_x(0)
         w_grouped = const.tile([P, H, PACK], BF16, align_bytes=64)
@@ -309,6 +359,9 @@ def tile_continuummemorysystem_pa_t_kernel(
             quantise_x(c)
         quantise_err(0)
         first_matmul(0)
+        for c in range(1, SCALAR_AHEAD):
+            transpose_err(c)
+            scalar_work(c)
 
         for c in range(N_CHUNKS + 1):
             if c + SCALAR_AHEAD + LOAD_AHEAD < N_CHUNKS:
@@ -316,11 +369,7 @@ def tile_continuummemorysystem_pa_t_kernel(
             if c >= 1:
                 quantise_d(c - 1)
                 second_matmuls(c - 1)
-            if c + SCALAR_AHEAD < N_CHUNKS:
-                transpose_err(c + SCALAR_AHEAD)
-            if c + SCALAR_AHEAD <= N_CHUNKS:
-                scalar_work(c + SCALAR_AHEAD)
-            if c + SCALAR_AHEAD == N_CHUNKS:
+            if c == N_CHUNKS - 2:
                 surprise_gate()
             if c < N_CHUNKS:
                 times_sigmoid(c)
@@ -328,6 +377,13 @@ def tile_continuummemorysystem_pa_t_kernel(
             if c + 1 < N_CHUNKS:
                 quantise_err(c + 1)
                 first_matmul(c + 1)
+            if c + SCALAR_AHEAD < N_CHUNKS:
+                transpose_err(c + SCALAR_AHEAD)
+                scalar_work(c + SCALAR_AHEAD)
+            if c + SCALAR_AHEAD == N_CHUNKS:
+                for late in range(N_CHUNKS - SQUARES_LATE, N_CHUNKS):
+                    square_err(late)
+                gram_diagonal()
             if c < N_CHUNKS:
                 d_up_val(c)
             if c + X_AHEAD < N_CHUNKS:

@@ -25,9 +25,9 @@ FLOPS = 3 * 2 * N_TOKENS * D * H
 SCALAR_AHEAD = 3
 X_AHEAD = 2
 LOAD_AHEAD = 2
-SQUARES_LATE = 3
+SQUARES_LATE = 4
 GRAM = P
-X_SHARE = 96
+X_SHARE = 128
 
 
 def tile_continuummemorysystem_pa_t_kernel(
@@ -128,8 +128,6 @@ def tile_continuummemorysystem_pa_t_kernel(
                     func=ACT.Tanh,
                     scale=0.5,
                 )
-                if c + 1 < N_CHUNKS:
-                    scalar_regroup_x(c + 1)
                 err_grouped = early.tile([P, K_PASS, PACK], BF16, align_bytes=64)
                 grouped_words = err_grouped[:].bitcast(F32)
                 for pair in range(PACK // 2):
@@ -142,6 +140,8 @@ def tile_continuummemorysystem_pa_t_kernel(
                 t["silu_neg"] = silu_neg
                 t["err_grouped"] = err_grouped
                 t["tanh_half"] = tanh_half
+            if c + 1 < N_CHUNKS:
+                scalar_regroup_x(c + 1)
             if c >= SQUARES_LATE:
                 square_err(c - SQUARES_LATE)
 
@@ -369,14 +369,14 @@ def tile_continuummemorysystem_pa_t_kernel(
             if c >= 1:
                 quantise_d(c - 1)
                 second_matmuls(c - 1)
-            if c == N_CHUNKS - 2:
-                surprise_gate()
             if c < N_CHUNKS:
                 times_sigmoid(c)
                 gate_slope(c)
             if c + 1 < N_CHUNKS:
                 quantise_err(c + 1)
                 first_matmul(c + 1)
+            if c == N_CHUNKS - 2:
+                surprise_gate()
             if c + SCALAR_AHEAD < N_CHUNKS:
                 transpose_err(c + SCALAR_AHEAD)
                 scalar_work(c + SCALAR_AHEAD)

from contextlib import ExitStack

import concourse.mybir as mybir
from concourse.masks import make_identity

F32 = mybir.dt.float32
BF16 = mybir.dt.bfloat16
U32 = mybir.dt.uint32
U8 = mybir.dt.uint8
FP8X4 = mybir.dt.float8_e4m3fn_x4
ACT = mybir.ActivationFunctionType
ALU = mybir.AluOpType

P = 128
PACK = 4
K_PASS = P * PACK

N_TOKENS = 8192
D = 512
H = 128
N_CHUNKS = N_TOKENS // K_PASS

FLOPS = 3 * 2 * N_TOKENS * D * H

SCALAR_AHEAD = 3
X_AHEAD = 2
LOAD_AHEAD = 2
SQUARES_LATE = 4
GRAM = P
X_SHARE = 128


def tile_continuummemorysystem_pa_t_kernel(
    tc, err, W_down, gate_pre, up_pre, x_pred, out_0, out_1
):
    nc = tc.nc
    with ExitStack() as ctx:
        const = ctx.enter_context(tc.tile_pool(name="const", bufs=1))
        inputs = ctx.enter_context(
            tc.tile_pool(name="inputs", bufs=LOAD_AHEAD + SCALAR_AHEAD + 2)
        )
        err_in = ctx.enter_context(
            tc.tile_pool(name="err_in", bufs=LOAD_AHEAD + SQUARES_LATE + 2)
        )
        early = ctx.enter_context(tc.tile_pool(name="early", bufs=SCALAR_AHEAD + 1))
        x_mx = ctx.enter_context(tc.tile_pool(name="x_mx", bufs=X_AHEAD + 2))
        work = ctx.enter_context(tc.tile_pool(name="work", bufs=2))
        psum_t = ctx.enter_context(tc.psum_pool(name="psum_t", bufs=4))
        psum_one = ctx.enter_context(tc.psum_pool(name="psum_one", bufs=1))
        ctx.enter_context(tc.manual_schedule())

        chunks = {}

        def token_rows(dram, c):
            return dram[c * K_PASS : (c + 1) * K_PASS, :].rearrange("(p j) f -> p j f", j=PACK)

        def side_by_side(grouped, rows):
            return (
                grouped.rearrange("p (c i) j -> p c j i", i=4),
                rows.rearrange("p j (c i) -> p c j i", i=4),
            )

        def load(c):
            x_sb = inputs.tile([P, PACK, D], BF16)
            nc.sync.dma_start(out=x_sb[:], in_=token_rows(x_pred, c))
            gate_sb = inputs.tile([P, PACK, H], BF16)
            nc.sync.dma_start(out=gate_sb[:], in_=token_rows(gate_pre, c))
            err_sb = err_in.tile([P, PACK, D], BF16)
            nc.sync.dma_start(out=err_sb[:], in_=token_rows(err, c))
            up_sb = inputs.tile([P, PACK, H], BF16)
            nc.sync.dma_start(out=up_sb[:], in_=token_rows(up_pre, c))
            chunks[c] = {"gate_sb": gate_sb, "err_sb": err_sb, "x_sb": x_sb, "up_sb": up_sb}

        def transpose_err(c):
            t = chunks[c]
            err_words = t["err_sb"][:].bitcast(F32)
            for pair in range(PACK // 2):
                err_t = psum_t.tile([P, 2, 2, P], F32, tag="err_t")
                for jj in range(2):
                    for u in range(2):
                        nc.tensor.transpose(
                            err_t[:, jj, u, :],
                            err_words[:, 2 * pair + jj, u * P : (u + 1) * P],
                            ident[:],
                        )
                t["err_t", pair] = err_t
            for j in range(PACK):
                nc.tensor.matmul(
                    out=gram[:],
                    lhsT=t["err_sb"][:, j, 0:GRAM],
                    rhs=t["err_sb"][:, j, 0:GRAM],
                    start=(c == 0 and j == 0),
                    stop=(c == N_CHUNKS - 1 and j == PACK - 1),
                )

        def scalar_regroup_x(c):
            t = chunks[c]
            x_grouped = early.tile([P, D, PACK], BF16, align_bytes=64)
            to_view, from_view = side_by_side(
                x_grouped[:, 0:X_SHARE, :], t["x_sb"][:, :, 0:X_SHARE]
            )
            nc.scalar.copy(out=to_view, in_=from_view)
            t["x_grouped"] = x_grouped

        def square_err(c):
            squares = work.tile([P, PACK, D - GRAM], BF16)
            nc.scalar.activation(
                out=squares[:],
                in_=chunks[c]["err_sb"][:, :, GRAM:D],
                func=ACT.Square,
                accum_out=sq_sums[:, c : c + 1],
            )

        def scalar_work(c):
            if c < N_CHUNKS:
                t = chunks[c]
                silu_neg = early.tile([P, H, PACK], F32)
                nc.scalar.activation(
                    out=silu_neg[:],
                    in_=t["gate_sb"][:].rearrange("p j h -> p h j"),
                    func=ACT.Silu,
                    scale=-1.0,
                )
                tanh_half = early.tile([P, H, PACK], F32)
                nc.scalar.activation(
                    out=tanh_half[:],
                    in_=t["gate_sb"][:].rearrange("p j h -> p h j"),
                    func=ACT.Tanh,
                    scale=0.5,
                )
                err_grouped = early.tile([P, K_PASS, PACK], BF16, align_bytes=64)
                grouped_words = err_grouped[:].bitcast(F32)
                for pair in range(PACK // 2):
                    nc.scalar.copy(
                        out=grouped_words[:, 2 * pair * P : 2 * (pair + 1) * P, :].rearrange(
                            "q (jj p) u -> q jj p u", jj=2
                        ),
                        in_=t["err_t", pair][:].rearrange("q jj u p -> q jj p u"),
                    )
                t["silu_neg"] = silu_neg
                t["err_grouped"] = err_grouped
                t["tanh_half"] = tanh_half
            if c + 1 < N_CHUNKS:
                scalar_regroup_x(c + 1)
            if c >= SQUARES_LATE:
                square_err(c - SQUARES_LATE)

        def quantise_err(c):
            t = chunks[c]
            err_codes = work.tile([P, K_PASS], U32, align_bytes=64)
            err_scales = work.tile([P, K_PASS], U8, align_bytes=64)
            nc.vector.quantize_mx(
                out=err_codes[:].bitcast(FP8X4),
                scales=err_scales[:],
                in_=t["err_grouped"][:].rearrange("q n s -> q (n s)"),
            )
            t["err_codes"] = err_codes
            t["err_scales"] = err_scales

        def first_matmul(c):
            t = chunks[c]
            dh = psum_one.tile([P, PACK, H], F32)
            for j in range(PACK):
                cols = slice(j * P, (j + 1) * P)
                nc.tensor.matmul_mx(
                    out=dh[:, j, :],
                    lhsT=t["err_codes"][:, cols].bitcast(FP8X4),
                    lhsT_scale=t["err_scales"][:, cols],
                    rhs=w_codes[:].bitcast(FP8X4),
                    rhs_scale=w_scales[:],
                    start=True,
                    stop=True,
                )
            t["dh"] = dh

        def regroup_x(c):
            t = chunks[c]
            to_view, from_view = side_by_side(
                t["x_grouped"][:, X_SHARE:D, :], t["x_sb"][:, :, X_SHARE:D]
            )
            nc.vector.tensor_copy(out=to_view, in_=from_view)

        def quantise_x(c):
            t = chunks[c]
            x_codes = x_mx.tile([P, D], U32, align_bytes=64)
            x_scales = x_mx.tile([P, D], U8, align_bytes=64)
            nc.vector.quantize_mx(
                out=x_codes[:].bitcast(FP8X4),
                scales=x_scales[:],
                in_=t["x_grouped"][:].rearrange("p d j -> p (d j)"),
            )
            t["x_codes"] = x_codes
            t["x_scales"] = x_scales

        def gate_slope(c):
            t = chunks[c]
            neg_slope = work.tile([P, H, PACK], F32)
            nc.vector.scalar_tensor_tensor(
                out=neg_slope[:],
                in0=t["silu_neg"][:],
                scalar=1.0,
                in1=t["up_sb"][:].rearrange("p j h -> p h j"),
                op0=ALU.subtract,
                op1=ALU.mult,
            )
            t["neg_slope"] = neg_slope

        def times_sigmoid(c):
            t = chunks[c]
            dh_sig2 = work.tile([P, H, PACK], F32)
            nc.vector.scalar_tensor_tensor(
                out=dh_sig2[:],
                in0=t["tanh_half"][:],
                scalar=1.0,
                in1=t["dh"][:].rearrange("p j h -> p h j"),
                op0=ALU.add,
                op1=ALU.mult,
            )
            t["dh_sig2"] = dh_sig2
            d_grouped = work.tile([P, 2, H, PACK], BF16, align_bytes=64)
            t["d_grouped"] = d_grouped

        def d_up_val(c):
            t = chunks[c]
            nc.vector.scalar_tensor_tensor(
                out=t["d_grouped"][:, 0],
                in0=t["dh_sig2"][:],
                scalar=0.5,
                in1=t["gate_sb"][:].rearrange("p j h -> p h j"),
                op0=ALU.mult,
                op1=ALU.mult,
            )

        def d_gate_pre(c):
            t = chunks[c]
            nc.vector.scalar_tensor_tensor(
                out=t["d_grouped"][:, 1],
                in0=t["dh_sig2"][:],
                scalar=-0.5,
                in1=t["neg_slope"][:],
                op0=ALU.mult,
                op1=ALU.mult,
            )

        def quantise_d(c):
            t = chunks[c]
            d_codes = work.tile([P, 2, H], U32, align_bytes=64)
            d_scales = work.tile([P, 2, H], U8, align_bytes=64)
            nc.vector.quantize_mx(
                out=d_codes[:].rearrange("p o h -> p (o h)").bitcast(FP8X4),
                scales=d_scales[:].rearrange("p o h -> p (o h)"),
                in_=t["d_grouped"][:].rearrange("p o h j -> p (o h j)"),
            )
            t["d_codes"] = d_codes
            t["d_scales"] = d_scales

        def second_matmuls(c):
            t = chunks[c]
            for o, acc in enumerate((acc_up, acc_gate)):
                nc.tensor.matmul_mx(
                    out=acc[:],
                    lhsT=t["d_codes"][:, o, :].bitcast(FP8X4),
                    lhsT_scale=t["d_scales"][:, o, :],
                    rhs=t["x_codes"][:].bitcast(FP8X4),
                    rhs_scale=t["x_scales"][:],
                    start=(c == 0),
                    stop=(c == N_CHUNKS - 1),
                )

        def gram_diagonal():
            diagonal = const.tile([P, GRAM], F32)
            nc.vector.tensor_tensor(out=diagonal[:], in0=gram[:], in1=ident[:], op=ALU.mult)
            nc.vector.tensor_reduce(
                out=sq_sums[:, N_CHUNKS : N_CHUNKS + 1],
                in_=diagonal[:],
                axis=mybir.AxisListType.X,
                op=ALU.add,
            )

        def surprise_gate():
            total_ps = psum_t.tile([P, N_CHUNKS + 1], F32, tag="err_t")
            nc.tensor.matmul(
                out=total_ps[:], lhsT=ones[:], rhs=sq_sums[:, 0 : N_CHUNKS + 1], start=True, stop=True
            )
            total_parts = const.tile([P, N_CHUNKS + 1], F32)
            mag_sq = const.tile([P, 1], F32)
            nc.scalar.activation(
                out=total_parts[:],
                in_=total_ps[:],
                func=ACT.Copy,
                scale=1.0 / (N_TOKENS * N_TOKENS),
                accum_out=mag_sq[:],
            )
            mag = const.tile([P, 1], F32)
            nc.gpsimd.tensor_tensor(out=mag[:], in0=mag_sq[:], in1=half[:], op=ALU.pow)
            ema = const.tile([P, 1], F32)
            nc.gpsimd.tensor_scalar(
                out=ema[:], in0=mag[:], scalar1=0.05, scalar2=0.95, op0=ALU.mult, op1=ALU.add
            )
            ema_floor = const.tile([P, 1], F32)
            nc.gpsimd.tensor_scalar_max(out=ema_floor[:], in0=ema[:], scalar1=1e-8)
            ema_inv = const.tile([P, 1], F32)
            nc.gpsimd.tensor_tensor(out=ema_inv[:], in0=ema_floor[:], in1=minus_one[:], op=ALU.pow)
            ratio = const.tile([P, 1], F32)
            nc.gpsimd.tensor_tensor(out=ratio[:], in0=mag[:], in1=ema_inv[:], op=ALU.mult)
            nc.gpsimd.tensor_scalar(
                out=gain[:],
                in0=ratio[:],
                scalar1=3.0,
                scalar2=1.0 / N_TOKENS,
                op0=ALU.min,
                op1=ALU.mult,
            )

        load(0)
        w_raw = const.tile([P, PACK, H], BF16)
        for u in range(2):
            nc.sync.dma_start(
                out=w_raw[:, 2 * u : 2 * u + 2, :],
                in_=W_down[256 * u : 256 * (u + 1), :].rearrange("(q e) h -> q e h", e=2),
            )
        for c in range(1, SCALAR_AHEAD + LOAD_AHEAD):
            load(c)

        ident = const.tile([P, P], F32)
        make_identity(nc, ident[:])
        ones = const.tile([P, P], F32)
        nc.gpsimd.memset(ones[:], 1.0)
        half = const.tile([P, 1], F32)
        nc.gpsimd.memset(half[:], 0.5)
        minus_one = const.tile([P, 1], F32)
        nc.gpsimd.memset(minus_one[:], -1.0)
        warm = const.tile([P, 1], F32)
        nc.scalar.activation(out=warm[:], in_=half[:], func=ACT.Silu)

        sq_sums = const.tile([P, N_CHUNKS + 8], F32)
        gain = const.tile([P, 1], F32)
        acc_up = psum_one.tile([P, D], F32)
        acc_gate = psum_one.tile([P, D], F32)
        gram = psum_one.tile([P, GRAM], F32)

        scalar_regroup_x(0)
        transpose_err(0)
        scalar_work(0)

        regroup_x(0)
        w_grouped = const.tile([P, H, PACK], BF16, align_bytes=64)
        nc.vector.tensor_copy(out=w_grouped[:], in_=w_raw[:].rearrange("q t h -> q h t"))
        quantise_x(0)
        w_codes = const.tile([P, H], U32, align_bytes=64)
        w_scales = const.tile([P, H], U8, align_bytes=64)
        nc.vector.quantize_mx(
            out=w_codes[:].bitcast(FP8X4),
            scales=w_scales[:],
            in_=w_grouped[:].rearrange("q h t -> q (h t)"),
        )
        for c in range(1, X_AHEAD):
            regroup_x(c)
            quantise_x(c)
        quantise_err(0)
        first_matmul(0)
        for c in range(1, SCALAR_AHEAD):
            transpose_err(c)
            scalar_work(c)

        for c in range(N_CHUNKS + 1):
            if c + SCALAR_AHEAD + LOAD_AHEAD < N_CHUNKS:
                load(c + SCALAR_AHEAD + LOAD_AHEAD)
            if c >= 1:
                quantise_d(c - 1)
                second_matmuls(c - 1)
            if c < N_CHUNKS:
                times_sigmoid(c)
                gate_slope(c)
            if c + 1 < N_CHUNKS:
                quantise_err(c + 1)
                first_matmul(c + 1)
            if c == N_CHUNKS - 2:
                surprise_gate()
            if c + SCALAR_AHEAD < N_CHUNKS:
                transpose_err(c + SCALAR_AHEAD)
                scalar_work(c + SCALAR_AHEAD)
            if c + SCALAR_AHEAD == N_CHUNKS:
                for late in range(N_CHUNKS - SQUARES_LATE, N_CHUNKS):
                    square_err(late)
                gram_diagonal()
            if c < N_CHUNKS:
                d_up_val(c)
            if c + X_AHEAD < N_CHUNKS:
                regroup_x(c + X_AHEAD)
            if c < N_CHUNKS:
                d_gate_pre(c)
            if c + X_AHEAD < N_CHUNKS:
                quantise_x(c + X_AHEAD)

        res_up = const.tile([P, D], F32)
        nc.scalar.activation(out=res_up[:], in_=acc_up[:], func=ACT.Copy, scale=gain[:, 0:1])
        nc.sync.dma_start(out=out_0, in_=res_up[:])
        res_gate = const.tile([P, D], F32)
        nc.vector.tensor_scalar_mul(out=res_gate[:], in0=acc_gate[:], scalar1=gain[:, 0:1])
        nc.sync.dma_start(out=out_1, in_=res_gate[:])
